import numpy as np
import ml_dtypes


def mxq(x, axis, fmt="e4m3"):
    dtype, down = {"e4m3": (ml_dtypes.float8_e4m3fn, 7), "e5m2": (ml_dtypes.float8_e5m2, 14)}[fmt]
    v = np.moveaxis(np.asarray(x, np.float32).astype(ml_dtypes.bfloat16).astype(np.float64), axis, -1)
    blocks = v.reshape(v.shape[:-1] + (-1, 32))
    amax = np.abs(blocks).max(-1, keepdims=True)
    byte = np.maximum(np.where(amax > 0, np.frexp(amax)[1] - 1 + 127, 0) - down, 1)
    scale = np.exp2(byte - 127.0)
    codes = (blocks / scale).astype(np.float32).astype(dtype).astype(np.float64)
    return np.moveaxis((codes * scale).reshape(v.shape), -1, axis)


WIDE = False


def mx_kscale(k):
    if not WIDE:
        return np.ones(k)
    levels = np.array([10, -10, 5, -5, 0])
    a = np.random.permutation(np.resize(levels, k // 512 * 4)).reshape(k // 512, 4)
    idx = np.arange(k)
    return np.exp2(a[idx // 512, idx % 128 // 32])


BF16 = ml_dtypes.bfloat16


def bf(x):
    return np.asarray(x, np.float32).astype(BF16)


def f64(x):
    return np.asarray(x).astype(np.float64)


B, N, DIM, H, KD, D = 32, 256, 512, 4, 16, 32
HD = 2 * KD + D
HQKV = H * HD
EPS = 1e-5


def setup_inputs():
    s = mx_kscale(DIM)
    c = 2.0 ** (-8.0 * np.random.random(HQKV))
    x = np.random.standard_normal((B, N, DIM)) + 0.5 * np.random.standard_normal(DIM)
    return {"x": bf(x * s),
            "qkv_w": bf(np.random.standard_normal((HQKV, DIM)) * c[:, None] / np.sqrt(DIM) / s),
            "qkv_g": bf(2.0 + 0.2 * np.random.standard_normal(HQKV)),
            "qkv_b": bf(0.3 * np.random.standard_normal(HQKV))}


def bn(y, g, b):
    m = y.mean(axis=(0, 1))
    v = ((y - m) ** 2).mean(axis=(0, 1))
    return (y - m) * (g / np.sqrt(v + EPS)) + b


def reference(x, qkv_w, qkv_g, qkv_b):
    y = mxq(f64(x), 2, "e4m3") @ mxq(f64(qkv_w), 1, "e4m3").T
    qkv = bn(y, f64(qkv_g), f64(qkv_b)).reshape(B, N, H, HD)
    q = qkv[..., :KD].transpose(0, 2, 1, 3)
    k = qkv[..., KD:2 * KD].transpose(0, 2, 1, 3)
    v = qkv[..., 2 * KD:].transpose(0, 2, 1, 3)
    return q, k, v

@@ -1,0 +1,263 @@
+from contextlib import ExitStack
+
+import concourse.mybir as mybir
+from concourse.masks import make_identity
+
+F32 = mybir.dt.float32
+BF16 = mybir.dt.bfloat16
+U32 = mybir.dt.uint32
+U8 = mybir.dt.uint8
+FP8X4 = mybir.dt.float8_e4m3fn_x4
+ACT = mybir.ActivationFunctionType
+ALU = mybir.AluOpType
+
+P = 128
+BATCHES, TOKENS, CHANNELS = 32, 256, 512
+HEADS, QK_DIM, V_DIM = 4, 16, 32
+HEAD_FEATURES = 2 * QK_DIM + V_DIM
+FEATURES = HEADS * HEAD_FEATURES
+HALVES = FEATURES // P
+ROWS = BATCHES * TOKENS
+EPS = 1e-5
+
+PACK = 4
+WORDS = CHANNELS // 2
+WORD_PLANES = WORDS // P
+
+BANK = 512
+UNIT_TOKENS = BANK // P
+GROUP_TOKENS = 8
+GROUP_UNITS = GROUP_TOKENS // UNIT_TOKENS
+GROUP_BATCHES = P * GROUP_TOKENS // TOKENS
+RUNS = TOKENS // GROUP_TOKENS
+UNITS = ROWS // BANK
+BN_STATS_DIM = 6
+LAG = 2
+
+PARTS = (
+    (0, QK_DIM, 0),
+    (QK_DIM, QK_DIM, HEADS * QK_DIM),
+    (2 * QK_DIM, V_DIM, 2 * HEADS * QK_DIM),
+)
+
+FLOPS = 2 * ROWS * CHANNELS * FEATURES
+
+
+def tile_attention_pa_t_kernel(tc, x, qkv_w, qkv_g, qkv_b, out_q, out_k, out_v):
+    nc = tc.nc
+    with ExitStack() as ctx:
+        const = ctx.enter_context(tc.tile_pool(name="const", bufs=1))
+        x_pool = ctx.enter_context(tc.tile_pool(name="x_rows", bufs=UNITS))
+        grouped_pool = ctx.enter_context(tc.tile_pool(name="grouped", bufs=3))
+        zt_pool = ctx.enter_context(tc.tile_pool(name="zt", bufs=HALVES * (LAG + 1)))
+        stage_pool = ctx.enter_context(tc.tile_pool(name="stage", bufs=3))
+        psum_t = ctx.enter_context(tc.psum_pool(name="psum_t", bufs=4))
+        psum_y = ctx.enter_context(tc.psum_pool(name="psum_y", bufs=4))
+        ctx.enter_context(tc.manual_schedule())
+
+        gb_rows = const.tile([P, FEATURES], BF16)
+        nc.vector.memset(gb_rows[:], 0.0)
+        nc.scalar.dma_start(out=gb_rows[0:1, :], in_=qkv_g.rearrange("(o f) -> o f", o=1))
+        nc.scalar.dma_start(out=gb_rows[1:2, :], in_=qkv_b.rearrange("(o f) -> o f", o=1))
+        w_rows = const.tile([P, HALVES * CHANNELS], BF16)
+        nc.sync.dma_start(
+            out=w_rows[:].rearrange("p (s k) -> p s k", s=HALVES),
+            in_=qkv_w.rearrange("(s p) k -> p s k", s=HALVES),
+        )
+        x_units = x.flatten_outer_dims().rearrange(
+            "(g p s t) k -> g s p (t k)", p=P, s=GROUP_UNITS, t=UNIT_TOKENS
+        )
+        x_rows = []
+        for unit in range(UNITS):
+            x_tile = x_pool.tile([P, UNIT_TOKENS * CHANNELS], BF16, name="x_tile")
+            nc.sync.dma_start(out=x_tile[:], in_=x_units[unit // GROUP_UNITS, unit % GROUP_UNITS])
+            x_rows.append(x_tile)
+
+        one = const.tile([P, 1], F32)
+        nc.vector.memset(one[:], 1.0)
+        table_warm = const.tile([P, 1], F32)
+        nc.scalar.activation(out=table_warm[:], in_=one[:], func=ACT.Sqrt)
+
+        identity = const.tile([P, P], F32)
+        make_identity(nc, identity[:])
+        row_order = const.tile([P, P], F32)
+        nc.vector.tensor_copy(
+            out=row_order[:].rearrange("p (r b) -> p r b", b=GROUP_BATCHES),
+            in_=identity[:].rearrange("p (b r) -> p r b", b=GROUP_BATCHES),
+        )
+
+        gb_sorted = const.tile([P, FEATURES], F32)
+        gb_by_head = gb_rows[:].rearrange("p (h j) -> p h j", h=HEADS)
+        for first, width, base in PARTS:
+            nc.vector.tensor_copy(
+                out=gb_sorted[:, base : base + HEADS * width].rearrange("p (h j) -> p h j", h=HEADS),
+                in_=gb_by_head[:, :, first : first + width],
+            )
+
+        w_words = w_rows[:].bitcast(F32)
+        wt = psum_t.tile([P, HALVES, WORD_PLANES, P], F32, tag="t")
+        for s in range(HALVES):
+            for u in range(WORD_PLANES):
+                first = (s * WORD_PLANES + u) * P
+                nc.tensor.transpose(wt[:, s, u, :], w_words[:, first : first + P], identity[:])
+        w_grouped = const.tile([P, FEATURES * PACK], BF16, align_bytes=64)
+        w_grouped_words = w_grouped[:].bitcast(F32).rearrange("p (f u) -> p f u", u=WORD_PLANES)
+        heads_here = HEADS // HALVES
+        for s in range(HALVES):
+            by_head = wt[:, s].rearrange("p u (h j) -> p h j u", h=heads_here)
+            for first, width, base in PARTS:
+                start = base + s * heads_here * width
+                nc.vector.tensor_copy(
+                    out=w_grouped_words[:, start : start + heads_here * width, :].rearrange(
+                        "p (h j) u -> p h j u", h=heads_here
+                    ),
+                    in_=by_head[:, :, first : first + width, :],
+                )
+        w_codes = const.tile([P, FEATURES], U32, align_bytes=64)
+        w_scales = const.tile([P, FEATURES], U8, align_bytes=64)
+        nc.vector.quantize_mx(out=w_codes[:].bitcast(FP8X4), scales=w_scales[:], in_=w_grouped[:])
+
+        gb_t = psum_t.tile([P, HALVES, P], F32, tag="t")
+        for half in range(HALVES):
+            nc.tensor.transpose(gb_t[:, half, :], gb_sorted[:, half * P : (half + 1) * P], identity[:])
+        gain_shift = const.tile([P, HALVES, 2], F32)
+        nc.vector.tensor_copy(out=gain_shift[:], in_=gb_t[:, :, 0:2])
+
+        x_codes = const.tile([P, ROWS], U32, align_bytes=64)
+        x_scales = const.tile([P, ROWS], U8, align_bytes=64)
+
+        def multiply(unit):
+            cols = slice(unit * BANK, (unit + 1) * BANK)
+            banks = []
+            for half in range(HALVES):
+                features = slice(half * P, (half + 1) * P)
+                y = psum_y.tile([P, BANK], F32, tag="y")
+                nc.tensor.matmul_mx(
+                    out=y[:],
+                    lhsT=w_codes[:, features].bitcast(FP8X4),
+                    lhsT_scale=w_scales[:, features],
+                    rhs=x_codes[:, cols].bitcast(FP8X4),
+                    rhs_scale=x_scales[:, cols],
+                    start=True,
+                    stop=True,
+                )
+                banks.append(y)
+            return banks
+
+        stats = const.tile([P, HALVES, UNITS, BN_STATS_DIM], F32)
+        grouped_of = {}
+
+        def transpose_x(unit):
+            words = x_rows[unit][:].bitcast(F32)
+            grouped = grouped_pool.tile([P, BANK * PACK], BF16, align_bytes=64)
+            grouped_words = grouped[:].bitcast(F32).rearrange(
+                "p (t c u) -> p t c u", t=UNIT_TOKENS, u=WORD_PLANES
+            )
+            tokens_per_bank = BANK // WORDS
+            for first_token in range(0, UNIT_TOKENS, tokens_per_bank):
+                xt = psum_t.tile([P, tokens_per_bank, WORD_PLANES, P], F32, tag="t")
+                for t in range(tokens_per_bank):
+                    for u in range(WORD_PLANES):
+                        first = ((first_token + t) * WORD_PLANES + u) * P
+                        nc.tensor.transpose(xt[:, t, u, :], words[:, first : first + P], row_order[:])
+                nc.scalar.copy(
+                    out=grouped_words[:, first_token : first_token + tokens_per_bank],
+                    in_=xt[:].rearrange("p t u c -> p t c u"),
+                )
+            grouped_of[unit] = grouped
+
+        def quantise_x(unit):
+            cols = slice(unit * BANK, (unit + 1) * BANK)
+            nc.vector.quantize_mx(
+                out=x_codes[:, cols].bitcast(FP8X4),
+                scales=x_scales[:, cols],
+                in_=grouped_of[unit][:],
+            )
+
+        def measure(unit):
+            for half, y in enumerate(multiply(unit)):
+                nc.vector.bn_stats(out=stats[:, half, unit, :], in_=y[:])
+
+        for step in range(UNITS + LAG):
+            if step < UNITS:
+                transpose_x(step)
+            if 1 <= step <= UNITS:
+                quantise_x(step - 1)
+            if step >= LAG:
+                measure(step - LAG)
+
+        mean_var = const.tile([P, HALVES, 2], F32)
+        for half in range(HALVES):
+            nc.vector.bn_aggr(
+                out=mean_var[:, half, :], in_=stats[:, half].rearrange("p u s -> p (u s)")
+            )
+        var_eps = const.tile([P, HALVES], F32)
+        nc.vector.tensor_scalar(
+            out=var_eps[:], in0=mean_var[:, :, 1], scalar1=EPS, scalar2=None, op0=ALU.add
+        )
+        std = const.tile([P, HALVES], F32)
+        nc.scalar.activation(out=std[:], in_=var_eps[:], func=ACT.Sqrt)
+        inv_std = const.tile([P, HALVES], F32)
+        nc.vector.reciprocal(out=inv_std[:], in_=std[:])
+        scale = const.tile([P, HALVES], F32)
+        nc.vector.tensor_tensor(out=scale[:], in0=gain_shift[:, :, 0], in1=inv_std[:], op=ALU.mult)
+        mean_scaled = const.tile([P, HALVES], F32)
+        nc.vector.tensor_tensor(out=mean_scaled[:], in0=mean_var[:, :, 0], in1=scale[:], op=ALU.mult)
+        shift = const.tile([P, HALVES], F32)
+        nc.vector.tensor_tensor(
+            out=shift[:], in0=gain_shift[:, :, 1], in1=mean_scaled[:], op=ALU.subtract
+        )
+
+        zt_of = {}
+        stage_of = {}
+
+        def normalise(unit):
+            tiles = []
+            for half, y in enumerate(multiply(unit)):
+                zt = zt_pool.tile([P, BANK], F32)
+                nc.scalar.activation(
+                    out=zt[:],
+                    in_=y[:],
+                    func=ACT.Identity,
+                    bias=shift[:, half : half + 1],
+                    scale=scale[:, half : half + 1],
+                )
+                tiles.append(zt)
+            zt_of[unit] = tiles
+
+        def collect(unit):
+            group, part = divmod(unit, GROUP_UNITS)
+            if part == 0:
+                stage_qk = stage_pool.tile([P, 2 * HEADS, GROUP_TOKENS, QK_DIM], F32)
+                stage_v = stage_pool.tile([P, HEADS, GROUP_TOKENS, V_DIM], F32)
+                stage_of[group] = (stage_qk, stage_v)
+            tokens = slice(part * UNIT_TOKENS, (part + 1) * UNIT_TOKENS)
+            for zt, stage, width in zip(zt_of[unit], stage_of[group], (QK_DIM, V_DIM)):
+                z = psum_t.tile([P, UNIT_TOKENS, P], F32, tag="t")
+                for t in range(UNIT_TOKENS):
+                    nc.tensor.transpose(z[:, t, :], zt[:, t * P : (t + 1) * P], identity[:])
+                nc.vector.tensor_copy(
+                    out=stage[:, :, tokens, :], in_=z[:].rearrange("p t (a j) -> p a t j", j=width)
+                )
+
+        def store(group):
+            stage_qk, stage_v = stage_of[group]
+            for b in range(GROUP_BATCHES):
+                batch = group * GROUP_BATCHES + b
+                for out, rows in (
+                    (out_q, stage_qk[b:P:GROUP_BATCHES, 0:HEADS]),
+                    (out_k, stage_qk[b:P:GROUP_BATCHES, HEADS : 2 * HEADS]),
+                    (out_v, stage_v[b:P:GROUP_BATCHES]),
+                ):
+                    nc.sync.dma_start(
+                        out=out[batch].rearrange("h (r t) j -> r h (t j)", t=GROUP_TOKENS),
+                        in_=rows.rearrange("p h t j -> p h (t j)"),
+                    )
+
+        for step in range(UNITS + LAG):
+            if step < UNITS:
+                normalise(step)
+            if step >= LAG:
+                collect(step - LAG)
+                if (step - LAG) % GROUP_UNITS == GROUP_UNITS - 1:
+                    store((step - LAG) // GROUP_UNITS)

@@ -49,7 +49,7 @@ def tile_attention_pa_t_kernel(tc, x, qkv_w, qkv_g, qkv_b, out_q, out_k, out_v):
         const = ctx.enter_context(tc.tile_pool(name="const", bufs=1))
         x_pool = ctx.enter_context(tc.tile_pool(name="x_rows", bufs=UNITS))
         grouped_pool = ctx.enter_context(tc.tile_pool(name="grouped", bufs=3))
-        zt_pool = ctx.enter_context(tc.tile_pool(name="zt", bufs=HALVES * (LAG + 1)))
+        zt_pool = ctx.enter_context(tc.tile_pool(name="zt", bufs=LAG + 1))
         stage_pool = ctx.enter_context(tc.tile_pool(name="stage", bufs=3))
         psum_t = ctx.enter_context(tc.psum_pool(name="psum_t", bufs=4))
         psum_y = ctx.enter_context(tc.psum_pool(name="psum_y", bufs=4))
@@ -212,18 +212,27 @@ def tile_attention_pa_t_kernel(tc, x, qkv_w, qkv_g, qkv_b, out_q, out_k, out_v):
         stage_of = {}
 
         def normalise(unit):
-            tiles = []
-            for half, y in enumerate(multiply(unit)):
-                zt = zt_pool.tile([P, BANK], F32)
-                nc.scalar.activation(
-                    out=zt[:],
-                    in_=y[:],
-                    func=ACT.Identity,
-                    bias=shift[:, half : half + 1],
-                    scale=scale[:, half : half + 1],
-                )
-                tiles.append(zt)
-            zt_of[unit] = tiles
+            y_qk, y_v = multiply(unit)
+            zt_qk = zt_pool.tile([P, BANK], F32)
+            nc.scalar.activation(
+                out=zt_qk[:], in_=y_qk[:], func=ACT.Identity, bias=shift[:, 0:1], scale=scale[:, 0:1]
+            )
+            zt_v = zt_pool.tile([P, BANK], F32)
+            nc.vector.tensor_scalar(
+                out=zt_v[:],
+                in0=y_v[:],
+                scalar1=scale[:, 1:2],
+                scalar2=shift[:, 1:2],
+                op0=ALU.mult,
+                op1=ALU.add,
+            )
+            zt_of[unit] = (zt_qk, zt_v)
+
+        def transpose_back(zt):
+            z = psum_t.tile([P, UNIT_TOKENS, P], F32, tag="t")
+            for t in range(UNIT_TOKENS):
+                nc.tensor.transpose(z[:, t, :], zt[:, t * P : (t + 1) * P], identity[:])
+            return z
 
         def collect(unit):
             group, part = divmod(unit, GROUP_UNITS)
@@ -231,14 +240,19 @@ def tile_attention_pa_t_kernel(tc, x, qkv_w, qkv_g, qkv_b, out_q, out_k, out_v):
                 stage_qk = stage_pool.tile([P, 2 * HEADS, GROUP_TOKENS, QK_DIM], F32)
                 stage_v = stage_pool.tile([P, HEADS, GROUP_TOKENS, V_DIM], F32)
                 stage_of[group] = (stage_qk, stage_v)
+            stage_qk, stage_v = stage_of[group]
+            zt_qk, zt_v = zt_of[unit]
             tokens = slice(part * UNIT_TOKENS, (part + 1) * UNIT_TOKENS)
-            for zt, stage, width in zip(zt_of[unit], stage_of[group], (QK_DIM, V_DIM)):
-                z = psum_t.tile([P, UNIT_TOKENS, P], F32, tag="t")
-                for t in range(UNIT_TOKENS):
-                    nc.tensor.transpose(z[:, t, :], zt[:, t * P : (t + 1) * P], identity[:])
-                nc.vector.tensor_copy(
-                    out=stage[:, :, tokens, :], in_=z[:].rearrange("p t (a j) -> p a t j", j=width)
-                )
+            z_qk = transpose_back(zt_qk)
+            z_v = transpose_back(zt_v)
+            nc.scalar.copy(
+                out=stage_qk[:, :, tokens, :],
+                in_=z_qk[:].rearrange("p t (a j) -> p a t j", j=QK_DIM),
+            )
+            nc.vector.tensor_copy(
+                out=stage_v[:, :, tokens, :],
+                in_=z_v[:].rearrange("p t (h j) -> p h t j", j=V_DIM),
+            )
 
         def store(group):
             stage_qk, stage_v = stage_of[group]

@@ -29,10 +29,9 @@ UNIT_TOKENS = BANK // P
 GROUP_TOKENS = 8
 GROUP_UNITS = GROUP_TOKENS // UNIT_TOKENS
 GROUP_BATCHES = P * GROUP_TOKENS // TOKENS
-RUNS = TOKENS // GROUP_TOKENS
 UNITS = ROWS // BANK
 BN_STATS_DIM = 6
-LAG = 2
+GROUPS = UNITS // GROUP_UNITS
 
 PARTS = (
     (0, QK_DIM, 0),
@@ -43,13 +42,17 @@ PARTS = (
 FLOPS = 2 * ROWS * CHANNELS * FEATURES
 
 
+def units_of(group):
+    return range(group * GROUP_UNITS, (group + 1) * GROUP_UNITS)
+
+
 def tile_attention_pa_t_kernel(tc, x, qkv_w, qkv_g, qkv_b, out_q, out_k, out_v):
     nc = tc.nc
     with ExitStack() as ctx:
         const = ctx.enter_context(tc.tile_pool(name="const", bufs=1))
         x_pool = ctx.enter_context(tc.tile_pool(name="x_rows", bufs=UNITS))
-        grouped_pool = ctx.enter_context(tc.tile_pool(name="grouped", bufs=3))
-        zt_pool = ctx.enter_context(tc.tile_pool(name="zt", bufs=LAG + 1))
+        grouped_pool = ctx.enter_context(tc.tile_pool(name="grouped", bufs=3 * GROUP_UNITS))
+        zt_pool = ctx.enter_context(tc.tile_pool(name="zt", bufs=2 * GROUP_UNITS))
         stage_pool = ctx.enter_context(tc.tile_pool(name="stage", bufs=3))
         psum_t = ctx.enter_context(tc.psum_pool(name="psum_t", bufs=4))
         psum_y = ctx.enter_context(tc.psum_pool(name="psum_y", bufs=4))
@@ -178,13 +181,16 @@ def tile_attention_pa_t_kernel(tc, x, qkv_w, qkv_g, qkv_b, out_q, out_k, out_v):
             for half, y in enumerate(multiply(unit)):
                 nc.vector.bn_stats(out=stats[:, half, unit, :], in_=y[:])
 
-        for step in range(UNITS + LAG):
-            if step < UNITS:
-                transpose_x(step)
-            if 1 <= step <= UNITS:
-                quantise_x(step - 1)
-            if step >= LAG:
-                measure(step - LAG)
+        for step in range(GROUPS + 2):
+            if step < GROUPS:
+                for unit in units_of(step):
+                    transpose_x(unit)
+            if 1 <= step <= GROUPS:
+                for unit in units_of(step - 1):
+                    quantise_x(unit)
+            if step >= 2:
+                for unit in units_of(step - 2):
+                    measure(unit)
 
         mean_var = const.tile([P, HALVES, 2], F32)
         for half in range(HALVES):
@@ -268,10 +274,11 @@ def tile_attention_pa_t_kernel(tc, x, qkv_w, qkv_g, qkv_b, out_q, out_k, out_v):
                         in_=rows.rearrange("p h t j -> p h (t j)"),
                     )
 
-        for step in range(UNITS + LAG):
-            if step < UNITS:
-                normalise(step)
-            if step >= LAG:
-                collect(step - LAG)
-                if (step - LAG) % GROUP_UNITS == GROUP_UNITS - 1:
-                    store((step - LAG) // GROUP_UNITS)
+        for step in range(GROUPS + 1):
+            if step < GROUPS:
+                for unit in units_of(step):
+                    normalise(unit)
+            if step >= 1:
+                for unit in units_of(step - 1):
+                    collect(unit)
+                store(step - 1)

from contextlib import ExitStack

import concourse.mybir as mybir
from concourse.masks import make_identity

F32 = mybir.dt.float32
BF16 = mybir.dt.bfloat16
U32 = mybir.dt.uint32
U8 = mybir.dt.uint8
FP8X4 = mybir.dt.float8_e4m3fn_x4
ACT = mybir.ActivationFunctionType
ALU = mybir.AluOpType

P = 128
BATCHES, TOKENS, CHANNELS = 32, 256, 512
HEADS, QK_DIM, V_DIM = 4, 16, 32
HEAD_FEATURES = 2 * QK_DIM + V_DIM
FEATURES = HEADS * HEAD_FEATURES
HALVES = FEATURES // P
ROWS = BATCHES * TOKENS
EPS = 1e-5

PACK = 4
WORDS = CHANNELS // 2
WORD_PLANES = WORDS // P

BANK = 512
UNIT_TOKENS = BANK // P
GROUP_TOKENS = 8
GROUP_UNITS = GROUP_TOKENS // UNIT_TOKENS
GROUP_BATCHES = P * GROUP_TOKENS // TOKENS
UNITS = ROWS // BANK
BN_STATS_DIM = 6
GROUPS = UNITS // GROUP_UNITS

PARTS = (
    (0, QK_DIM, 0),
    (QK_DIM, QK_DIM, HEADS * QK_DIM),
    (2 * QK_DIM, V_DIM, 2 * HEADS * QK_DIM),
)

FLOPS = 2 * ROWS * CHANNELS * FEATURES


def units_of(group):
    return range(group * GROUP_UNITS, (group + 1) * GROUP_UNITS)


def tile_attention_pa_t_kernel(tc, x, qkv_w, qkv_g, qkv_b, out_q, out_k, out_v):
    nc = tc.nc
    with ExitStack() as ctx:
        const = ctx.enter_context(tc.tile_pool(name="const", bufs=1))
        x_pool = ctx.enter_context(tc.tile_pool(name="x_rows", bufs=UNITS))
        grouped_pool = ctx.enter_context(tc.tile_pool(name="grouped", bufs=3 * GROUP_UNITS))
        zt_pool = ctx.enter_context(tc.tile_pool(name="zt", bufs=2 * GROUP_UNITS))
        stage_pool = ctx.enter_context(tc.tile_pool(name="stage", bufs=3))
        psum_t = ctx.enter_context(tc.psum_pool(name="psum_t", bufs=4))
        psum_y = ctx.enter_context(tc.psum_pool(name="psum_y", bufs=4))
        ctx.enter_context(tc.manual_schedule())

        gb_rows = const.tile([P, FEATURES], BF16)
        nc.vector.memset(gb_rows[:], 0.0)
        nc.scalar.dma_start(out=gb_rows[0:1, :], in_=qkv_g.rearrange("(o f) -> o f", o=1))
        nc.scalar.dma_start(out=gb_rows[1:2, :], in_=qkv_b.rearrange("(o f) -> o f", o=1))
        w_rows = const.tile([P, HALVES * CHANNELS], BF16)
        nc.sync.dma_start(
            out=w_rows[:].rearrange("p (s k) -> p s k", s=HALVES),
            in_=qkv_w.rearrange("(s p) k -> p s k", s=HALVES),
        )
        x_units = x.flatten_outer_dims().rearrange(
            "(g p s t) k -> g s p (t k)", p=P, s=GROUP_UNITS, t=UNIT_TOKENS
        )
        x_rows = []
        for unit in range(UNITS):
            x_tile = x_pool.tile([P, UNIT_TOKENS * CHANNELS], BF16, name="x_tile")
            nc.sync.dma_start(out=x_tile[:], in_=x_units[unit // GROUP_UNITS, unit % GROUP_UNITS])
            x_rows.append(x_tile)

        one = const.tile([P, 1], F32)
        nc.vector.memset(one[:], 1.0)
        table_warm = const.tile([P, 1], F32)
        nc.scalar.activation(out=table_warm[:], in_=one[:], func=ACT.Sqrt)

        identity = const.tile([P, P], F32)
        make_identity(nc, identity[:])
        row_order = const.tile([P, P], F32)
        nc.vector.tensor_copy(
            out=row_order[:].rearrange("p (r b) -> p r b", b=GROUP_BATCHES),
            in_=identity[:].rearrange("p (b r) -> p r b", b=GROUP_BATCHES),
        )

        gb_sorted = const.tile([P, FEATURES], F32)
        gb_by_head = gb_rows[:].rearrange("p (h j) -> p h j", h=HEADS)
        for first, width, base in PARTS:
            nc.vector.tensor_copy(
                out=gb_sorted[:, base : base + HEADS * width].rearrange("p (h j) -> p h j", h=HEADS),
                in_=gb_by_head[:, :, first : first + width],
            )

        w_words = w_rows[:].bitcast(F32)
        wt = psum_t.tile([P, HALVES, WORD_PLANES, P], F32, tag="t")
        for s in range(HALVES):
            for u in range(WORD_PLANES):
                first = (s * WORD_PLANES + u) * P
                nc.tensor.transpose(wt[:, s, u, :], w_words[:, first : first + P], identity[:])
        w_grouped = const.tile([P, FEATURES * PACK], BF16, align_bytes=64)
        w_grouped_words = w_grouped[:].bitcast(F32).rearrange("p (f u) -> p f u", u=WORD_PLANES)
        heads_here = HEADS // HALVES
        for s in range(HALVES):
            by_head = wt[:, s].rearrange("p u (h j) -> p h j u", h=heads_here)
            for first, width, base in PARTS:
                start = base + s * heads_here * width
                nc.vector.tensor_copy(
                    out=w_grouped_words[:, start : start + heads_here * width, :].rearrange(
                        "p (h j) u -> p h j u", h=heads_here
                    ),
                    in_=by_head[:, :, first : first + width, :],
                )
        w_codes = const.tile([P, FEATURES], U32, align_bytes=64)
        w_scales = const.tile([P, FEATURES], U8, align_bytes=64)
        nc.vector.quantize_mx(out=w_codes[:].bitcast(FP8X4), scales=w_scales[:], in_=w_grouped[:])

        gb_t = psum_t.tile([P, HALVES, P], F32, tag="t")
        for half in range(HALVES):
            nc.tensor.transpose(gb_t[:, half, :], gb_sorted[:, half * P : (half + 1) * P], identity[:])
        gain_shift = const.tile([P, HALVES, 2], F32)
        nc.vector.tensor_copy(out=gain_shift[:], in_=gb_t[:, :, 0:2])

        x_codes = const.tile([P, ROWS], U32, align_bytes=64)
        x_scales = const.tile([P, ROWS], U8, align_bytes=64)

        def multiply(unit):
            cols = slice(unit * BANK, (unit + 1) * BANK)
            banks = []
            for half in range(HALVES):
                features = slice(half * P, (half + 1) * P)
                y = psum_y.tile([P, BANK], F32, tag="y")
                nc.tensor.matmul_mx(
                    out=y[:],
                    lhsT=w_codes[:, features].bitcast(FP8X4),
                    lhsT_scale=w_scales[:, features],
                    rhs=x_codes[:, cols].bitcast(FP8X4),
                    rhs_scale=x_scales[:, cols],
                    start=True,
                    stop=True,
                )
                banks.append(y)
            return banks

        stats = const.tile([P, HALVES, UNITS, BN_STATS_DIM], F32)
        grouped_of = {}

        def transpose_x(unit):
            words = x_rows[unit][:].bitcast(F32)
            grouped = grouped_pool.tile([P, BANK * PACK], BF16, align_bytes=64)
            grouped_words = grouped[:].bitcast(F32).rearrange(
                "p (t c u) -> p t c u", t=UNIT_TOKENS, u=WORD_PLANES
            )
            tokens_per_bank = BANK // WORDS
            for first_token in range(0, UNIT_TOKENS, tokens_per_bank):
                xt = psum_t.tile([P, tokens_per_bank, WORD_PLANES, P], F32, tag="t")
                for t in range(tokens_per_bank):
                    for u in range(WORD_PLANES):
                        first = ((first_token + t) * WORD_PLANES + u) * P
                        nc.tensor.transpose(xt[:, t, u, :], words[:, first : first + P], row_order[:])
                nc.scalar.copy(
                    out=grouped_words[:, first_token : first_token + tokens_per_bank],
                    in_=xt[:].rearrange("p t u c -> p t c u"),
                )
            grouped_of[unit] = grouped

        def quantise_x(unit):
            cols = slice(unit * BANK, (unit + 1) * BANK)
            nc.vector.quantize_mx(
                out=x_codes[:, cols].bitcast(FP8X4),
                scales=x_scales[:, cols],
                in_=grouped_of[unit][:],
            )

        def measure(unit):
            for half, y in enumerate(multiply(unit)):
                nc.vector.bn_stats(out=stats[:, half, unit, :], in_=y[:])

        for step in range(GROUPS + 2):
            if step < GROUPS:
                for unit in units_of(step):
                    transpose_x(unit)
            if 1 <= step <= GROUPS:
                for unit in units_of(step - 1):
                    quantise_x(unit)
            if step >= 2:
                for unit in units_of(step - 2):
                    measure(unit)

        mean_var = const.tile([P, HALVES, 2], F32)
        for half in range(HALVES):
            nc.vector.bn_aggr(
                out=mean_var[:, half, :], in_=stats[:, half].rearrange("p u s -> p (u s)")
            )
        var_eps = const.tile([P, HALVES], F32)
        nc.vector.tensor_scalar(
            out=var_eps[:], in0=mean_var[:, :, 1], scalar1=EPS, scalar2=None, op0=ALU.add
        )
        std = const.tile([P, HALVES], F32)
        nc.scalar.activation(out=std[:], in_=var_eps[:], func=ACT.Sqrt)
        inv_std = const.tile([P, HALVES], F32)
        nc.vector.reciprocal(out=inv_std[:], in_=std[:])
        scale = const.tile([P, HALVES], F32)
        nc.vector.tensor_tensor(out=scale[:], in0=gain_shift[:, :, 0], in1=inv_std[:], op=ALU.mult)
        mean_scaled = const.tile([P, HALVES], F32)
        nc.vector.tensor_tensor(out=mean_scaled[:], in0=mean_var[:, :, 0], in1=scale[:], op=ALU.mult)
        shift = const.tile([P, HALVES], F32)
        nc.vector.tensor_tensor(
            out=shift[:], in0=gain_shift[:, :, 1], in1=mean_scaled[:], op=ALU.subtract
        )

        zt_of = {}
        stage_of = {}

        def normalise(unit):
            y_qk, y_v = multiply(unit)
            zt_qk = zt_pool.tile([P, BANK], F32)
            nc.scalar.activation(
                out=zt_qk[:], in_=y_qk[:], func=ACT.Identity, bias=shift[:, 0:1], scale=scale[:, 0:1]
            )
            zt_v = zt_pool.tile([P, BANK], F32)
            nc.vector.tensor_scalar(
                out=zt_v[:],
                in0=y_v[:],
                scalar1=scale[:, 1:2],
                scalar2=shift[:, 1:2],
                op0=ALU.mult,
                op1=ALU.add,
            )
            zt_of[unit] = (zt_qk, zt_v)

        def transpose_back(zt):
            z = psum_t.tile([P, UNIT_TOKENS, P], F32, tag="t")
            for t in range(UNIT_TOKENS):
                nc.tensor.transpose(z[:, t, :], zt[:, t * P : (t + 1) * P], identity[:])
            return z

        def collect(unit):
            group, part = divmod(unit, GROUP_UNITS)
            if part == 0:
                stage_qk = stage_pool.tile([P, 2 * HEADS, GROUP_TOKENS, QK_DIM], F32)
                stage_v = stage_pool.tile([P, HEADS, GROUP_TOKENS, V_DIM], F32)
                stage_of[group] = (stage_qk, stage_v)
            stage_qk, stage_v = stage_of[group]
            zt_qk, zt_v = zt_of[unit]
            tokens = slice(part * UNIT_TOKENS, (part + 1) * UNIT_TOKENS)
            z_qk = transpose_back(zt_qk)
            z_v = transpose_back(zt_v)
            nc.scalar.copy(
                out=stage_qk[:, :, tokens, :],
                in_=z_qk[:].rearrange("p t (a j) -> p a t j", j=QK_DIM),
            )
            nc.vector.tensor_copy(
                out=stage_v[:, :, tokens, :],
                in_=z_v[:].rearrange("p t (h j) -> p h t j", j=V_DIM),
            )

        def store(group):
            stage_qk, stage_v = stage_of[group]
            for b in range(GROUP_BATCHES):
                batch = group * GROUP_BATCHES + b
                for out, rows in (
                    (out_q, stage_qk[b:P:GROUP_BATCHES, 0:HEADS]),
                    (out_k, stage_qk[b:P:GROUP_BATCHES, HEADS : 2 * HEADS]),
                    (out_v, stage_v[b:P:GROUP_BATCHES]),
                ):
                    nc.sync.dma_start(
                        out=out[batch].rearrange("h (r t) j -> r h (t j)", t=GROUP_TOKENS),
                        in_=rows.rearrange("p h t j -> p h (t j)"),
                    )

        for step in range(GROUPS + 1):
            if step < GROUPS:
                for unit in units_of(step):
                    normalise(unit)
            if step >= 1:
                for unit in units_of(step - 1):
                    collect(unit)
                store(step - 1)
